import numpy as np
import ml_dtypes


def mxq(x, axis, fmt="e4m3"):
    dtype, down = {"e4m3": (ml_dtypes.float8_e4m3fn, 7), "e5m2": (ml_dtypes.float8_e5m2, 14)}[fmt]
    v = np.moveaxis(np.asarray(x, np.float32).astype(ml_dtypes.bfloat16).astype(np.float64), axis, -1)
    blocks = v.reshape(v.shape[:-1] + (-1, 32))
    amax = np.abs(blocks).max(-1, keepdims=True)
    byte = np.maximum(np.where(amax > 0, np.frexp(amax)[1] - 1 + 127, 0) - down, 1)
    scale = np.exp2(byte - 127.0)
    codes = (blocks / scale).astype(np.float32).astype(dtype).astype(np.float64)
    return np.moveaxis((codes * scale).reshape(v.shape), -1, axis)


WIDE = False


def mx_kscale(k):
    if not WIDE:
        return np.ones(k)
    levels = np.array([10, -10, 5, -5, 0])
    a = np.random.permutation(np.resize(levels, k // 512 * 4)).reshape(k // 512, 4)
    idx = np.arange(k)
    return np.exp2(a[idx // 512, idx % 128 // 32])


BF16 = ml_dtypes.bfloat16


def bf(x):
    return np.asarray(x, np.float32).astype(BF16)


def f64(x):
    return np.asarray(x).astype(np.float64)


B, N, F, G, K = 4, 512, 512, 512, 2048
EPS = 1e-8


def setup_inputs():
    s = mx_kscale(F)
    a = np.random.standard_normal((B, N, 1))
    g = np.random.standard_normal((B, 1, F))
    h = 2.0 * (np.random.standard_normal((B, N, F)) + a * g)
    w = (np.random.standard_normal((F, G)) + 0.5 * np.random.standard_normal((F, 1))) / np.sqrt(F)
    return {"h": bf(h * s), "W_h": bf(w / s[:, None]), "beta": bf(2.0 + np.random.uniform(size=1))}


def reference(h, W_h, beta):
    Wh = mxq(f64(h), 2, "e4m3") @ mxq(f64(W_h), 0, "e4m3")
    xm = Wh - Wh.mean(-1, keepdims=True)
    xq = mxq(xm, 2, "e4m3")
    cov = xq @ xq.transpose(0, 2, 1)
    norm = np.sqrt((xm * xm).sum(-1))
    denom = norm[:, :, None] * norm[:, None, :] + EPS
    return f64(beta) * np.abs(cov / denom)

@@ -1,0 +1,321 @@
+from contextlib import ExitStack
+
+import concourse.mybir as mybir
+from concourse.masks import make_identity
+
+F32 = mybir.dt.float32
+BF16 = mybir.dt.bfloat16
+U32 = mybir.dt.uint32
+U8 = mybir.dt.uint8
+FP8X4 = mybir.dt.float8_e4m3fn_x4
+ACT = mybir.ActivationFunctionType
+ALU = mybir.AluOpType
+
+P = 128
+PACK = 4
+GRAPHS = 4
+NODES = 512
+FEATS_IN = 512
+FEATS = 512
+BLOCKS = NODES // P
+MX_WIDTHS = (128, 256, 512)
+EPS = 1e-8
+TINY = 1e-30
+
+FLOPS = 2 * GRAPHS * NODES * FEATS_IN * FEATS + 2 * GRAPHS * NODES * NODES * FEATS
+
+
+def tile_pearsonattention_pa_kernel(tc, h, W_h, beta, out):
+    nc = tc.nc
+    with ExitStack() as ctx:
+        const = ctx.enter_context(tc.tile_pool(name="const", bufs=1))
+        halves = ctx.enter_context(tc.tile_pool(name="halves", bufs=2 * GRAPHS))
+        graph = ctx.enter_context(tc.tile_pool(name="graph", bufs=GRAPHS))
+        ps_bc = ctx.enter_context(tc.psum_pool(name="ps_bc", bufs=1))
+        ps_acc = ctx.enter_context(tc.psum_pool(name="ps_acc", bufs=6))
+
+        w_raw = const.tile([P, PACK, FEATS], BF16)
+        nc.sync.dma_start(
+            out=w_raw[:].rearrange("p (u e) g -> p u e g", u=2),
+            in_=W_h.rearrange("(u p e) g -> p u e g", u=2, e=2),
+        )
+        beta_bf = const.tile([P, 1], BF16)
+        nc.scalar.dma_start(out=beta_bf[:], in_=beta.partition_broadcast(P))
+        h_raw = []
+        for b in range(GRAPHS):
+            for half in range(2):
+                raw = halves.tile([P, 2 * FEATS_IN], BF16, name="h_raw")
+                nc.sync.dma_start(
+                    out=raw[:].rearrange("p (j k) -> p j k", j=2),
+                    in_=h[b, half * 2 * P : (half + 1) * 2 * P, :].rearrange("(j p) k -> p j k", p=P),
+                )
+                h_raw.append(raw)
+
+        ident = const.tile([P, P], F32)
+        make_identity(nc, ident[:])
+        eps_col = const.tile([P, 1], F32)
+        nc.vector.memset(eps_col[:], EPS)
+        tiny_col = const.tile([P, 1], F32)
+        nc.vector.memset(tiny_col[:], TINY)
+        beta_col = const.tile([P, 1], F32)
+        nc.gpsimd.tensor_copy(out=beta_col[:], in_=beta_bf[:])
+        warm = const.tile([P, 1], F32)
+        nc.scalar.activation(out=warm[:], in_=eps_col[:], func=ACT.Abs_reciprocal_sqrt)
+
+        w_grp = const.tile([P, FEATS, PACK], BF16, align_bytes=64)
+        nc.vector.tensor_copy(
+            out=w_grp[:].rearrange("p (tg pg) t -> p tg pg t", tg=PACK),
+            in_=w_raw[:].rearrange("p t (pg tg) -> p tg pg t", tg=PACK),
+        )
+        w_codes = const.tile([P, FEATS], U32, align_bytes=64)
+        w_scales = const.tile([P, FEATS], U8, align_bytes=64)
+        nc.vector.quantize_mx(
+            out=w_codes[:].bitcast(FP8X4),
+            scales=w_scales[:],
+            in_=w_grp[:].rearrange("p c t -> p (c t)"),
+        )
+
+        state = [dict() for b in range(GRAPHS)]
+
+        def transpose_h(b):
+            banks = []
+            for half in range(2):
+                words = h_raw[2 * b + half][:].bitcast(F32).rearrange("p (j u w) -> p j u w", j=2, u=2)
+                h_t = ps_acc.tile([P, 2, 2, P], F32, tag="acc")
+                for j in range(2):
+                    for u in range(2):
+                        nc.tensor.transpose(h_t[:, j, u, :], words[:, j, u, :], ident[:])
+                banks.append(h_t)
+            state[b]["h_t"] = banks
+
+        def group_h(b):
+            h_grp = graph.tile([P, NODES * PACK], BF16, align_bytes=64)
+            grp_words = h_grp[:].bitcast(F32).rearrange("p (r n u) -> p r n u", r=BLOCKS, u=2)
+            for half in range(2):
+                nc.scalar.copy(
+                    out=grp_words[:, 2 * half : 2 * half + 2, :, :],
+                    in_=state[b]["h_t"][half][:].rearrange("p j u n -> p j n u"),
+                )
+            state[b]["h_grp"] = h_grp
+
+        def quantise_h(b):
+            h_codes = graph.tile([P, NODES], U32, align_bytes=64)
+            h_scales = graph.tile([P, NODES], U8, align_bytes=64)
+            for half in range(2):
+                cols = slice(half * 2 * P, (half + 1) * 2 * P)
+                nc.vector.quantize_mx(
+                    out=h_codes[:, cols].bitcast(FP8X4),
+                    scales=h_scales[:, cols],
+                    in_=state[b]["h_grp"][:, half * 2 * P * PACK : (half + 1) * 2 * P * PACK],
+                )
+            state[b]["h_codes"] = h_codes
+            state[b]["h_scales"] = h_scales
+
+        def node_stats(b):
+            st = state[b]
+            stats = graph.tile([P, BLOCKS, 6], F32)
+            mean_var = graph.tile([P, BLOCKS, 2], F32)
+            for r in range(BLOCKS):
+                cols = slice(r * P, (r + 1) * P)
+                wh = ps_acc.tile([P, FEATS], F32, tag="acc")
+                nc.tensor.matmul_mx(
+                    out=wh[:],
+                    lhsT=st["h_codes"][:, cols].bitcast(FP8X4),
+                    lhsT_scale=st["h_scales"][:, cols],
+                    rhs=w_codes[:].bitcast(FP8X4),
+                    rhs_scale=w_scales[:],
+                    start=True,
+                    stop=True,
+                )
+                nc.vector.bn_stats(out=stats[:, r, :], in_=wh[:])
+                nc.vector.bn_aggr(out=mean_var[:, r, :], in_=stats[:, r, :])
+            st["mean_var"] = mean_var
+
+        def inverse_norm(b):
+            inv_norm = graph.tile([P, BLOCKS], F32)
+            nc.scalar.activation(
+                out=inv_norm[:],
+                in_=state[b]["mean_var"][:, :, 1],
+                func=ACT.Abs_reciprocal_sqrt,
+                scale=float(FEATS),
+                bias=tiny_col[:],
+            )
+            state[b]["inv_norm"] = inv_norm
+
+        def node_norm(b):
+            norm = graph.tile([P, BLOCKS], F32)
+            nc.vector.scalar_tensor_tensor(
+                out=norm[:],
+                in0=state[b]["mean_var"][:, :, 1],
+                scalar=float(FEATS),
+                in1=state[b]["inv_norm"][:],
+                op0=ALU.mult,
+                op1=ALU.mult,
+            )
+            state[b]["norm"] = norm
+
+        def spread(b):
+            st = state[b]
+            mean_ps = ps_bc.tile([P, NODES], F32)
+            norm_ps = ps_bc.tile([P, NODES], F32)
+            for r in range(BLOCKS):
+                nc.tensor.transpose(
+                    mean_ps[:, r * P : (r + 1) * P], st["mean_var"][:, r, 0:1].to_broadcast([P, P]), ident[:]
+                )
+            for r in range(BLOCKS):
+                nc.tensor.transpose(
+                    norm_ps[:, r * P : (r + 1) * P], st["norm"][:, r : r + 1].to_broadcast([P, P]), ident[:]
+                )
+            st["mean_ps"] = mean_ps
+            st["norm_ps"] = norm_ps
+
+        def copy_mean(b):
+            mean_bc = graph.tile([P, NODES], F32)
+            nc.scalar.copy(out=mean_bc[:], in_=state[b]["mean_ps"][:])
+            state[b]["mean_bc"] = mean_bc
+
+        def upper(r):
+            return slice(r * P, NODES)
+
+        def inverse_denominator(b):
+            st = state[b]
+            inv_root = graph.tile([P, BLOCKS, NODES], F32)
+            inv_denom = graph.tile([P, BLOCKS, NODES], F32)
+            for r in range(BLOCKS):
+                nc.scalar.activation(
+                    out=inv_root[:, r, upper(r)],
+                    in_=st["norm_ps"][:, upper(r)],
+                    func=ACT.Abs_reciprocal_sqrt,
+                    scale=st["norm"][:, r : r + 1],
+                    bias=eps_col[:],
+                )
+            for r in range(BLOCKS):
+                nc.scalar.activation(
+                    out=inv_denom[:, r, upper(r)], in_=inv_root[:, r, upper(r)], func=ACT.Square
+                )
+            for r in range(0, BLOCKS, 2):
+                nc.gpsimd.tensor_scalar(
+                    out=inv_denom[:, r, upper(r)],
+                    in0=inv_denom[:, r, upper(r)],
+                    scalar1=beta_col[:, 0:1],
+                    scalar2=0.0,
+                    op0=ALU.mult,
+                    op1=ALU.add,
+                )
+            st["inv_denom"] = inv_denom
+
+        def centre(b):
+            st = state[b]
+            x_grp = graph.tile([P, NODES, PACK], BF16, align_bytes=64)
+            for r in range(BLOCKS):
+                cols = slice(r * P, (r + 1) * P)
+                wh_t = ps_acc.tile([P, PACK, P], F32, tag="acc")
+                for tg in range(PACK):
+                    g_cols = slice(tg * P, (tg + 1) * P)
+                    nc.tensor.matmul_mx(
+                        out=wh_t[:, tg, :],
+                        lhsT=w_codes[:, g_cols].bitcast(FP8X4),
+                        lhsT_scale=w_scales[:, g_cols],
+                        rhs=st["h_codes"][:, cols].bitcast(FP8X4),
+                        rhs_scale=st["h_scales"][:, cols],
+                        start=True,
+                        stop=True,
+                    )
+                nc.vector.tensor_tensor(
+                    out=x_grp[:, cols, :],
+                    in0=wh_t[:].rearrange("p t n -> p n t"),
+                    in1=st["mean_bc"][:, cols].unsqueeze(2).to_broadcast([P, P, PACK]),
+                    op=ALU.subtract,
+                )
+            st["x_grp"] = x_grp
+
+        def quantise_x(b):
+            x_codes = graph.tile([P, NODES], U32, align_bytes=64)
+            x_scales = graph.tile([P, NODES], U8, align_bytes=64)
+            nc.vector.quantize_mx(
+                out=x_codes[:].bitcast(FP8X4),
+                scales=x_scales[:],
+                in_=state[b]["x_grp"][:].rearrange("p n t -> p (n t)"),
+            )
+            state[b]["x_codes"] = x_codes
+            state[b]["x_scales"] = x_scales
+
+        def correlate(b):
+            st = state[b]
+            result = graph.tile([P, BLOCKS, NODES], F32)
+            out_rows = out[b].rearrange("(r p) m -> p r m", p=P)
+            for r in range(BLOCKS):
+                needed = NODES - r * P
+                width = min([n for n in MX_WIDTHS if n >= needed])
+                cov = ps_acc.tile([P, width], F32, tag="acc")
+                nc.tensor.matmul_mx(
+                    out=cov[:],
+                    lhsT=st["x_codes"][:, r * P : (r + 1) * P].bitcast(FP8X4),
+                    lhsT_scale=st["x_scales"][:, r * P : (r + 1) * P],
+                    rhs=st["x_codes"][:, NODES - width :].bitcast(FP8X4),
+                    rhs_scale=st["x_scales"][:, NODES - width :],
+                    start=True,
+                    stop=True,
+                )
+                nc.scalar.activation(out=result[:, r, upper(r)], in_=cov[:, width - needed :], func=ACT.Abs)
+                if r % 2 == 0:
+                    multiplier = nc.gpsimd if b + 1 < GRAPHS else nc.vector
+                    multiplier.tensor_tensor(
+                        out=result[:, r, upper(r)],
+                        in0=result[:, r, upper(r)],
+                        in1=st["inv_denom"][:, r, upper(r)],
+                        op=ALU.mult,
+                    )
+                else:
+                    nc.vector.scalar_tensor_tensor(
+                        out=result[:, r, upper(r)],
+                        in0=result[:, r, upper(r)],
+                        scalar=beta_col[:, 0:1],
+                        in1=st["inv_denom"][:, r, upper(r)],
+                        op0=ALU.mult,
+                        op1=ALU.mult,
+                    )
+            nc.sync.dma_start(out=out_rows[:, 0, :], in_=result[:, 0, :])
+            st["result"] = result
+
+        def mirror(b):
+            result = state[b]["result"]
+            out_rows = out[b].rearrange("(r p) m -> p r m", p=P)
+            for c in range(1, BLOCKS):
+                mirror = ps_acc.tile([P, c * P], F32, tag="acc")
+                for r in range(c):
+                    nc.tensor.transpose(
+                        mirror[:, r * P : (r + 1) * P], result[:, r, c * P : (c + 1) * P], ident[:]
+                    )
+                nc.scalar.copy(out=result[:, c, 0 : c * P], in_=mirror[:])
+                nc.sync.dma_start(out=out_rows[:, c, :], in_=result[:, c, :])
+
+        def live(b):
+            return 0 <= b < GRAPHS
+
+        for s in range(-2, GRAPHS + 3):
+            if live(s - 3):
+                mirror(s - 3)
+            if live(s - 1):
+                copy_mean(s - 1)
+            if live(s + 1):
+                group_h(s + 1)
+            if live(s - 1):
+                inverse_denominator(s - 1)
+            if live(s):
+                node_stats(s)
+                inverse_norm(s)
+            if live(s + 1):
+                quantise_h(s + 1)
+            if live(s):
+                node_norm(s)
+            if live(s - 1):
+                centre(s - 1)
+            if live(s - 2):
+                correlate(s - 2)
+            if live(s - 1):
+                quantise_x(s - 1)
+            if live(s + 2):
+                transpose_h(s + 2)
+            if live(s):
+                spread(s)

@@ -193,15 +193,6 @@ def tile_pearsonattention_pa_kernel(tc, h, W_h, beta, out):
                 nc.scalar.activation(
                     out=inv_denom[:, r, upper(r)], in_=inv_root[:, r, upper(r)], func=ACT.Square
                 )
-            for r in range(0, BLOCKS, 2):
-                nc.gpsimd.tensor_scalar(
-                    out=inv_denom[:, r, upper(r)],
-                    in0=inv_denom[:, r, upper(r)],
-                    scalar1=beta_col[:, 0:1],
-                    scalar2=0.0,
-                    op0=ALU.mult,
-                    op1=ALU.add,
-                )
             st["inv_denom"] = inv_denom
 
         def centre(b):
@@ -258,23 +249,14 @@ def tile_pearsonattention_pa_kernel(tc, h, W_h, beta, out):
                     stop=True,
                 )
                 nc.scalar.activation(out=result[:, r, upper(r)], in_=cov[:, width - needed :], func=ACT.Abs)
-                if r % 2 == 0:
-                    multiplier = nc.gpsimd if b + 1 < GRAPHS else nc.vector
-                    multiplier.tensor_tensor(
-                        out=result[:, r, upper(r)],
-                        in0=result[:, r, upper(r)],
-                        in1=st["inv_denom"][:, r, upper(r)],
-                        op=ALU.mult,
-                    )
-                else:
-                    nc.vector.scalar_tensor_tensor(
-                        out=result[:, r, upper(r)],
-                        in0=result[:, r, upper(r)],
-                        scalar=beta_col[:, 0:1],
-                        in1=st["inv_denom"][:, r, upper(r)],
-                        op0=ALU.mult,
-                        op1=ALU.mult,
-                    )
+                nc.vector.scalar_tensor_tensor(
+                    out=result[:, r, upper(r)],
+                    in0=result[:, r, upper(r)],
+                    scalar=beta_col[:, 0:1],
+                    in1=st["inv_denom"][:, r, upper(r)],
+                    op0=ALU.mult,
+                    op1=ALU.mult,
+                )
             nc.sync.dma_start(out=out_rows[:, 0, :], in_=result[:, 0, :])
             st["result"] = result
 

@@ -18,9 +18,15 @@ NODES = 512
 FEATS_IN = 512
 FEATS = 512
 BLOCKS = NODES // P
-MX_WIDTHS = (128, 256, 512)
+HALF = NODES // 2
+W_SPLIT = 80
 EPS = 1e-8
 TINY = 1e-30
+
+BANKS = ((0,), (1, 3), (2,))
+FIRST = {0: 0, 1: 512, 3: 896, 2: 1024}
+TRI = 1280
+MOVING = {0: ((0, 512),), 1: ((128, 384), (384, 512)), 2: ((256, 512),), 3: ((384, 512),)}
 
 FLOPS = 2 * GRAPHS * NODES * FEATS_IN * FEATS + 2 * GRAPHS * NODES * NODES * FEATS
 
@@ -31,8 +37,9 @@ def tile_pearsonattention_pa_kernel(tc, h, W_h, beta, out):
         const = ctx.enter_context(tc.tile_pool(name="const", bufs=1))
         halves = ctx.enter_context(tc.tile_pool(name="halves", bufs=2 * GRAPHS))
         graph = ctx.enter_context(tc.tile_pool(name="graph", bufs=GRAPHS))
+        ps_v = ctx.enter_context(tc.psum_pool(name="ps_v", bufs=3))
+        ps_s = ctx.enter_context(tc.psum_pool(name="ps_s", bufs=3))
         ps_bc = ctx.enter_context(tc.psum_pool(name="ps_bc", bufs=1))
-        ps_acc = ctx.enter_context(tc.psum_pool(name="ps_acc", bufs=6))
 
         w_raw = const.tile([P, PACK, FEATS], BF16)
         nc.sync.dma_start(
@@ -47,7 +54,7 @@ def tile_pearsonattention_pa_kernel(tc, h, W_h, beta, out):
                 raw = halves.tile([P, 2 * FEATS_IN], BF16, name="h_raw")
                 nc.sync.dma_start(
                     out=raw[:].rearrange("p (j k) -> p j k", j=2),
-                    in_=h[b, half * 2 * P : (half + 1) * 2 * P, :].rearrange("(j p) k -> p j k", p=P),
+                    in_=h[b, half * HALF : (half + 1) * HALF, :].rearrange("(j p) k -> p j k", p=P),
                 )
                 h_raw.append(raw)
 
@@ -63,10 +70,10 @@ def tile_pearsonattention_pa_kernel(tc, h, W_h, beta, out):
         nc.scalar.activation(out=warm[:], in_=eps_col[:], func=ACT.Abs_reciprocal_sqrt)
 
         w_grp = const.tile([P, FEATS, PACK], BF16, align_bytes=64)
-        nc.vector.tensor_copy(
-            out=w_grp[:].rearrange("p (tg pg) t -> p tg pg t", tg=PACK),
-            in_=w_raw[:].rearrange("p t (pg tg) -> p tg pg t", tg=PACK),
-        )
+        w_to = w_grp[:].rearrange("p (tg pg) t -> p tg pg t", tg=PACK)
+        w_from = w_raw[:].rearrange("p t (pg tg) -> p tg pg t", tg=PACK)
+        nc.vector.tensor_copy(out=w_to[:, :, 0:W_SPLIT, :], in_=w_from[:, :, 0:W_SPLIT, :])
+        nc.scalar.copy(out=w_to[:, :, W_SPLIT:, :], in_=w_from[:, :, W_SPLIT:, :])
         w_codes = const.tile([P, FEATS], U32, align_bytes=64)
         w_scales = const.tile([P, FEATS], U8, align_bytes=64)
         nc.vector.quantize_mx(
@@ -75,229 +82,290 @@ def tile_pearsonattention_pa_kernel(tc, h, W_h, beta, out):
             in_=w_grp[:].rearrange("p c t -> p (c t)"),
         )
 
-        state = [dict() for b in range(GRAPHS)]
+        state = []
+        for b in range(GRAPHS):
+            st = dict()
+            st["h_grp"] = graph.tile([P, NODES * PACK], BF16, name="h_grp", align_bytes=64)
+            st["h_codes"] = graph.tile([P, NODES], U32, name="h_codes", align_bytes=64)
+            st["h_scales"] = graph.tile([P, NODES], U8, name="h_scales", align_bytes=64)
+            st["stats"] = graph.tile([P, BLOCKS, 6], F32, name="stats")
+            st["twice_mean"] = graph.tile([P, BLOCKS], F32, name="twice_mean")
+            st["gap"] = graph.tile([P, BLOCKS], F32, name="gap")
+            st["sumsq"] = graph.tile([P, BLOCKS], F32, name="sumsq")
+            st["inv_norm"] = graph.tile([P, BLOCKS], F32, name="inv_norm")
+            st["norm"] = graph.tile([P, BLOCKS], F32, name="norm")
+            st["mean_bc"] = graph.tile([P, NODES], F32, name="mean_bc")
+            st["inv_root"] = graph.tile([P, TRI], F32, name="inv_root")
+            st["inv_denom"] = graph.tile([P, TRI], F32, name="inv_denom")
+            st["x_grp"] = graph.tile([P, NODES, PACK], BF16, name="x_grp", align_bytes=64)
+            st["x_codes"] = graph.tile([P, NODES], U32, name="x_codes", align_bytes=64)
+            st["x_scales"] = graph.tile([P, NODES], U8, name="x_scales", align_bytes=64)
+            st["magnitude"] = graph.tile([P, TRI], F32, name="magnitude")
+            st["result"] = graph.tile([P, BLOCKS, NODES], F32, name="result")
+            state.append(st)
 
-        def transpose_h(b):
-            banks = []
-            for half in range(2):
-                words = h_raw[2 * b + half][:].bitcast(F32).rearrange("p (j u w) -> p j u w", j=2, u=2)
-                h_t = ps_acc.tile([P, 2, 2, P], F32, tag="acc")
-                for j in range(2):
-                    for u in range(2):
-                        nc.tensor.transpose(h_t[:, j, u, :], words[:, j, u, :], ident[:])
-                banks.append(h_t)
-            state[b]["h_t"] = banks
+        def block(r):
+            return slice(r * P, (r + 1) * P)
 
-        def group_h(b):
-            h_grp = graph.tile([P, NODES * PACK], BF16, align_bytes=64)
-            grp_words = h_grp[:].bitcast(F32).rearrange("p (r n u) -> p r n u", r=BLOCKS, u=2)
-            for half in range(2):
-                nc.scalar.copy(
-                    out=grp_words[:, 2 * half : 2 * half + 2, :, :],
-                    in_=state[b]["h_t"][half][:].rearrange("p j u n -> p j n u"),
-                )
-            state[b]["h_grp"] = h_grp
+        def tri(r):
+            return slice(FIRST[r], FIRST[r] + NODES - r * P)
 
-        def quantise_h(b):
-            h_codes = graph.tile([P, NODES], U32, align_bytes=64)
-            h_scales = graph.tile([P, NODES], U8, align_bytes=64)
-            for half in range(2):
-                cols = slice(half * 2 * P, (half + 1) * 2 * P)
-                nc.vector.quantize_mx(
-                    out=h_codes[:, cols].bitcast(FP8X4),
-                    scales=h_scales[:, cols],
-                    in_=state[b]["h_grp"][:, half * 2 * P * PACK : (half + 1) * 2 * P * PACK],
-                )
-            state[b]["h_codes"] = h_codes
-            state[b]["h_scales"] = h_scales
+        def transpose_h(b, half):
+            words = h_raw[2 * b + half][:].bitcast(F32).rearrange("p (j u w) -> p j u w", j=2, u=2)
+            h_t = ps_s.tile([P, 2, 2, P], F32, tag="s")
+            for j in range(2):
+                for u in range(2):
+                    nc.tensor.transpose(h_t[:, j, u, :], words[:, j, u, :], ident[:])
+            state[b]["h_t", half] = h_t
 
-        def node_stats(b):
+        def group_h(b, half):
+            grp_words = state[b]["h_grp"][:].bitcast(F32).rearrange("p (r n u) -> p r n u", r=BLOCKS, u=2)
+            nc.scalar.copy(
+                out=grp_words[:, 2 * half : 2 * half + 2, :, :],
+                in_=state[b]["h_t", half][:].rearrange("p j u n -> p j n u"),
+            )
+
+        def quantise_h(b, half):
             st = state[b]
-            stats = graph.tile([P, BLOCKS, 6], F32)
-            mean_var = graph.tile([P, BLOCKS, 2], F32)
-            for r in range(BLOCKS):
-                cols = slice(r * P, (r + 1) * P)
-                wh = ps_acc.tile([P, FEATS], F32, tag="acc")
-                nc.tensor.matmul_mx(
-                    out=wh[:],
-                    lhsT=st["h_codes"][:, cols].bitcast(FP8X4),
-                    lhsT_scale=st["h_scales"][:, cols],
-                    rhs=w_codes[:].bitcast(FP8X4),
-                    rhs_scale=w_scales[:],
-                    start=True,
-                    stop=True,
-                )
-                nc.vector.bn_stats(out=stats[:, r, :], in_=wh[:])
-                nc.vector.bn_aggr(out=mean_var[:, r, :], in_=stats[:, r, :])
-            st["mean_var"] = mean_var
+            cols = slice(half * HALF, (half + 1) * HALF)
+            nc.vector.quantize_mx(
+                out=st["h_codes"][:, cols].bitcast(FP8X4),
+                scales=st["h_scales"][:, cols],
+                in_=st["h_grp"][:, half * HALF * PACK : (half + 1) * HALF * PACK],
+            )
 
-        def inverse_norm(b):
-            inv_norm = graph.tile([P, BLOCKS], F32)
+        def project(b, r):
+            st = state[b]
+            wh = ps_v.tile([P, FEATS], F32, tag="v")
+            nc.tensor.matmul_mx(
+                out=wh[:],
+                lhsT=st["h_codes"][:, block(r)].bitcast(FP8X4),
+                lhsT_scale=st["h_scales"][:, block(r)],
+                rhs=w_codes[:].bitcast(FP8X4),
+                rhs_scale=w_scales[:],
+                start=True,
+                stop=True,
+            )
+            st["wh", r] = wh
+
+        def node_stats(b, r):
+            nc.vector.bn_stats(out=state[b]["stats"][:, r, :], in_=state[b]["wh", r][:])
+
+        def mean(b):
+            stats = state[b]["stats"]
+            nc.vector.tensor_tensor(
+                out=state[b]["twice_mean"][:], in0=stats[:, :, 1], in1=stats[:, :, 4], op=ALU.add
+            )
+
+        def norm(b):
+            st = state[b]
+            stats, gap, sumsq = st["stats"], st["gap"], st["sumsq"]
+            nc.gpsimd.tensor_tensor(out=gap[:], in0=stats[:, :, 1], in1=stats[:, :, 4], op=ALU.subtract)
+            nc.gpsimd.tensor_tensor(out=sumsq[:], in0=stats[:, :, 2], in1=stats[:, :, 5], op=ALU.add)
+            nc.gpsimd.tensor_tensor(out=gap[:], in0=gap[:], in1=gap[:], op=ALU.mult)
+            nc.gpsimd.tensor_scalar(
+                out=gap[:], in0=gap[:], scalar1=float(FEATS // 4), scalar2=0.0, op0=ALU.mult, op1=ALU.add
+            )
+            nc.gpsimd.tensor_tensor(out=sumsq[:], in0=sumsq[:], in1=gap[:], op=ALU.add)
             nc.scalar.activation(
-                out=inv_norm[:],
-                in_=state[b]["mean_var"][:, :, 1],
-                func=ACT.Abs_reciprocal_sqrt,
-                scale=float(FEATS),
-                bias=tiny_col[:],
+                out=st["inv_norm"][:], in_=sumsq[:], func=ACT.Abs_reciprocal_sqrt, bias=tiny_col[:]
             )
-            state[b]["inv_norm"] = inv_norm
+            nc.gpsimd.tensor_tensor(out=st["norm"][:], in0=sumsq[:], in1=st["inv_norm"][:], op=ALU.mult)
 
-        def node_norm(b):
-            norm = graph.tile([P, BLOCKS], F32)
-            nc.vector.scalar_tensor_tensor(
-                out=norm[:],
-                in0=state[b]["mean_var"][:, :, 1],
-                scalar=float(FEATS),
-                in1=state[b]["inv_norm"][:],
-                op0=ALU.mult,
-                op1=ALU.mult,
-            )
-            state[b]["norm"] = norm
-
-        def spread(b):
-            st = state[b]
-            mean_ps = ps_bc.tile([P, NODES], F32)
-            norm_ps = ps_bc.tile([P, NODES], F32)
+        def spread(b, what):
+            bank = ps_bc.tile([P, NODES], F32, name="spread_" + what)
             for r in range(BLOCKS):
                 nc.tensor.transpose(
-                    mean_ps[:, r * P : (r + 1) * P], st["mean_var"][:, r, 0:1].to_broadcast([P, P]), ident[:]
+                    bank[:, block(r)], state[b][what][:, r : r + 1].to_broadcast([P, P]), ident[:]
                 )
-            for r in range(BLOCKS):
-                nc.tensor.transpose(
-                    norm_ps[:, r * P : (r + 1) * P], st["norm"][:, r : r + 1].to_broadcast([P, P]), ident[:]
-                )
-            st["mean_ps"] = mean_ps
-            st["norm_ps"] = norm_ps
+            state[b]["spread_" + what] = bank
 
         def copy_mean(b):
-            mean_bc = graph.tile([P, NODES], F32)
-            nc.scalar.copy(out=mean_bc[:], in_=state[b]["mean_ps"][:])
-            state[b]["mean_bc"] = mean_bc
+            nc.scalar.activation(
+                out=state[b]["mean_bc"][:], in_=state[b]["spread_twice_mean"][:], func=ACT.Copy, scale=0.5
+            )
 
-        def upper(r):
-            return slice(r * P, NODES)
-
-        def inverse_denominator(b):
+        def inverse_root(b):
             st = state[b]
-            inv_root = graph.tile([P, BLOCKS, NODES], F32)
-            inv_denom = graph.tile([P, BLOCKS, NODES], F32)
             for r in range(BLOCKS):
                 nc.scalar.activation(
-                    out=inv_root[:, r, upper(r)],
-                    in_=st["norm_ps"][:, upper(r)],
+                    out=st["inv_root"][:, tri(r)],
+                    in_=st["spread_norm"][:, r * P :],
                     func=ACT.Abs_reciprocal_sqrt,
                     scale=st["norm"][:, r : r + 1],
                     bias=eps_col[:],
                 )
-            for r in range(BLOCKS):
-                nc.scalar.activation(
-                    out=inv_denom[:, r, upper(r)], in_=inv_root[:, r, upper(r)], func=ACT.Square
-                )
-            st["inv_denom"] = inv_denom
 
-        def centre(b):
+        def inverse_denominator(b):
+            nc.scalar.activation(out=state[b]["inv_denom"][:], in_=state[b]["inv_root"][:], func=ACT.Square)
+
+        def project_t(b, r):
             st = state[b]
-            x_grp = graph.tile([P, NODES, PACK], BF16, align_bytes=64)
-            for r in range(BLOCKS):
-                cols = slice(r * P, (r + 1) * P)
-                wh_t = ps_acc.tile([P, PACK, P], F32, tag="acc")
-                for tg in range(PACK):
-                    g_cols = slice(tg * P, (tg + 1) * P)
-                    nc.tensor.matmul_mx(
-                        out=wh_t[:, tg, :],
-                        lhsT=w_codes[:, g_cols].bitcast(FP8X4),
-                        lhsT_scale=w_scales[:, g_cols],
-                        rhs=st["h_codes"][:, cols].bitcast(FP8X4),
-                        rhs_scale=st["h_scales"][:, cols],
-                        start=True,
-                        stop=True,
-                    )
-                nc.vector.tensor_tensor(
-                    out=x_grp[:, cols, :],
-                    in0=wh_t[:].rearrange("p t n -> p n t"),
-                    in1=st["mean_bc"][:, cols].unsqueeze(2).to_broadcast([P, P, PACK]),
-                    op=ALU.subtract,
-                )
-            st["x_grp"] = x_grp
-
-        def quantise_x(b):
-            x_codes = graph.tile([P, NODES], U32, align_bytes=64)
-            x_scales = graph.tile([P, NODES], U8, align_bytes=64)
-            nc.vector.quantize_mx(
-                out=x_codes[:].bitcast(FP8X4),
-                scales=x_scales[:],
-                in_=state[b]["x_grp"][:].rearrange("p n t -> p (n t)"),
-            )
-            state[b]["x_codes"] = x_codes
-            state[b]["x_scales"] = x_scales
-
-        def correlate(b):
-            st = state[b]
-            result = graph.tile([P, BLOCKS, NODES], F32)
-            out_rows = out[b].rearrange("(r p) m -> p r m", p=P)
-            for r in range(BLOCKS):
-                needed = NODES - r * P
-                width = min([n for n in MX_WIDTHS if n >= needed])
-                cov = ps_acc.tile([P, width], F32, tag="acc")
+            wh_t = ps_v.tile([P, PACK, P], F32, tag="v")
+            for tg in range(PACK):
                 nc.tensor.matmul_mx(
-                    out=cov[:],
-                    lhsT=st["x_codes"][:, r * P : (r + 1) * P].bitcast(FP8X4),
-                    lhsT_scale=st["x_scales"][:, r * P : (r + 1) * P],
-                    rhs=st["x_codes"][:, NODES - width :].bitcast(FP8X4),
-                    rhs_scale=st["x_scales"][:, NODES - width :],
+                    out=wh_t[:, tg, :],
+                    lhsT=w_codes[:, block(tg)].bitcast(FP8X4),
+                    lhsT_scale=w_scales[:, block(tg)],
+                    rhs=st["h_codes"][:, block(r)].bitcast(FP8X4),
+                    rhs_scale=st["h_scales"][:, block(r)],
                     start=True,
                     stop=True,
                 )
-                nc.scalar.activation(out=result[:, r, upper(r)], in_=cov[:, width - needed :], func=ACT.Abs)
-                nc.vector.scalar_tensor_tensor(
-                    out=result[:, r, upper(r)],
-                    in0=result[:, r, upper(r)],
-                    scalar=beta_col[:, 0:1],
-                    in1=st["inv_denom"][:, r, upper(r)],
-                    op0=ALU.mult,
-                    op1=ALU.mult,
-                )
-            nc.sync.dma_start(out=out_rows[:, 0, :], in_=result[:, 0, :])
-            st["result"] = result
+            st["wh_t", r] = wh_t
 
-        def mirror(b):
-            result = state[b]["result"]
-            out_rows = out[b].rearrange("(r p) m -> p r m", p=P)
-            for c in range(1, BLOCKS):
-                mirror = ps_acc.tile([P, c * P], F32, tag="acc")
-                for r in range(c):
-                    nc.tensor.transpose(
-                        mirror[:, r * P : (r + 1) * P], result[:, r, c * P : (c + 1) * P], ident[:]
+        def centre(b, r):
+            st = state[b]
+            nc.vector.tensor_tensor(
+                out=st["x_grp"][:, block(r), :],
+                in0=st["wh_t", r][:].rearrange("p t n -> p n t"),
+                in1=st["mean_bc"][:, block(r)].unsqueeze(2).to_broadcast([P, P, PACK]),
+                op=ALU.subtract,
+            )
+
+        def quantise_x(b):
+            st = state[b]
+            nc.vector.quantize_mx(
+                out=st["x_codes"][:].bitcast(FP8X4),
+                scales=st["x_scales"][:],
+                in_=st["x_grp"][:].rearrange("p n t -> p (n t)"),
+            )
+
+        def covariance(b, i):
+            st = state[b]
+            start = FIRST[BANKS[i][0]]
+            cov = ps_s.tile([P, sum([NODES - r * P for r in BANKS[i]])], F32, tag="s")
+            for r in BANKS[i]:
+                for m0, m1 in MOVING[r]:
+                    at = FIRST[r] - start + m0 - r * P
+                    nc.tensor.matmul_mx(
+                        out=cov[:, at : at + m1 - m0],
+                        lhsT=st["x_codes"][:, block(r)].bitcast(FP8X4),
+                        lhsT_scale=st["x_scales"][:, block(r)],
+                        rhs=st["x_codes"][:, m0:m1].bitcast(FP8X4),
+                        rhs_scale=st["x_scales"][:, m0:m1],
+                        start=True,
+                        stop=True,
                     )
-                nc.scalar.copy(out=result[:, c, 0 : c * P], in_=mirror[:])
-                nc.sync.dma_start(out=out_rows[:, c, :], in_=result[:, c, :])
+            st["cov", i] = cov
+
+        def absolute(b, i):
+            start = FIRST[BANKS[i][0]]
+            width = sum([NODES - r * P for r in BANKS[i]])
+            nc.scalar.activation(
+                out=state[b]["magnitude"][:, start : start + width], in_=state[b]["cov", i][:], func=ACT.Abs
+            )
+
+        def scale(b, r):
+            st = state[b]
+            nc.vector.scalar_tensor_tensor(
+                out=st["result"][:, r, r * P :],
+                in0=st["magnitude"][:, tri(r)],
+                scalar=beta_col[:, 0:1],
+                in1=st["inv_denom"][:, tri(r)],
+                op0=ALU.mult,
+                op1=ALU.mult,
+            )
+
+        def store(b, r):
+            nc.sync.dma_start(out=out[b, r * P : (r + 1) * P, :], in_=state[b]["result"][:, r, :])
+
+        def mirror(b, c):
+            bank = ps_s.tile([P, c * P], F32, tag="s")
+            for r in range(c):
+                nc.tensor.transpose(bank[:, block(r)], state[b]["result"][:, r, block(c)], ident[:])
+            state[b]["mirror", c] = bank
+
+        def copy_mirror(b, c):
+            out_cols = state[b]["result"][:, c, 0 : c * P]
+            if b + 1 == GRAPHS and c == 2:
+                nc.vector.tensor_copy(out=out_cols, in_=state[b]["mirror", c][:])
+            else:
+                nc.scalar.copy(out=out_cols, in_=state[b]["mirror", c][:])
+            store(b, c)
 
         def live(b):
             return 0 <= b < GRAPHS
 
-        for s in range(-2, GRAPHS + 3):
-            if live(s - 3):
-                mirror(s - 3)
-            if live(s - 1):
-                copy_mean(s - 1)
-            if live(s + 1):
-                group_h(s + 1)
-            if live(s - 1):
-                inverse_denominator(s - 1)
-            if live(s):
-                node_stats(s)
-                inverse_norm(s)
-            if live(s + 1):
-                quantise_h(s + 1)
-            if live(s):
-                node_norm(s)
-            if live(s - 1):
-                centre(s - 1)
-            if live(s - 2):
-                correlate(s - 2)
-            if live(s - 1):
-                quantise_x(s - 1)
-            if live(s + 2):
-                transpose_h(s + 2)
-            if live(s):
-                spread(s)
+        with tc.manual_schedule():
+            for s in range(-3, GRAPHS + 3):
+                if live(s - 1):
+                    inverse_denominator(s - 1)
+                if live(s - 3):
+                    for c in range(1, BLOCKS):
+                        copy_mirror(s - 3, c)
+                if live(s):
+                    copy_mean(s)
+                    inverse_root(s)
+                if live(s + 3) and s + 3 != 1:
+                    for half in range(2):
+                        transpose_h(s + 3, half)
+                    for half in range(2):
+                        group_h(s + 3, half)
+                if live(s):
+                    if s < GRAPHS - 1:
+                        project_t(s, 2)
+                    project_t(s, 3)
+                if live(s - 2):
+                    for c in range(1, BLOCKS):
+                        mirror(s - 2, c)
+                if live(s):
+                    centre(s, 0)
+                    if live(s + 1):
+                        mean(s + 1)
+                    for r in range(1, BLOCKS):
+                        centre(s, r)
+                if live(s + 2):
+                    quantise_h(s + 2, 0)
+                    if s == -1:
+                        mean(0)
+                    quantise_h(s + 2, 1)
+                if live(s + 1):
+                    spread(s + 1, "twice_mean")
+                if live(s - 1):
+                    for i in range(len(BANKS)):
+                        absolute(s - 1, i)
+                if live(s + 1):
+                    norm(s + 1)
+                if live(s + 2):
+                    for r in range(3):
+                        project(s + 2, r)
+                    if s + 3 == 1:
+                        for half in range(2):
+                            transpose_h(1, half)
+                        for half in range(2):
+                            group_h(1, half)
+                    if live(s + 1):
+                        spread(s + 1, "norm")
+                    if live(s):
+                        quantise_x(s)
+                        for i in range(len(BANKS)):
+                            covariance(s, i)
+                    node_stats(s + 2, 0)
+                    project(s + 2, 3)
+                    node_stats(s + 2, 1)
+                    if live(s + 1):
+                        project_t(s + 1, 0)
+                    node_stats(s + 2, 2)
+                    if live(s + 1):
+                        project_t(s + 1, 1)
+                    node_stats(s + 2, 3)
+                    if live(s - 1):
+                        for r in (0, 1, 3, 2):
+                            scale(s - 1, r)
+                        store(s - 1, 0)
+                else:
+                    if live(s + 1):
+                        for r in range(3):
+                            project_t(s + 1, r)
+                        spread(s + 1, "norm")
+                    if live(s - 1):
+                        scale(s - 1, 0)
+                        store(s - 1, 0)
+                    if live(s):
+                        quantise_x(s)
+                        for i in range(len(BANKS)):
+                            covariance(s, i)
+                    if live(s - 1):
+                        for r in (1, 3, 2):
+                            scale(s - 1, r)

@@ -89,11 +89,10 @@ def tile_pearsonattention_pa_kernel(tc, h, W_h, beta, out):
             st["h_codes"] = graph.tile([P, NODES], U32, name="h_codes", align_bytes=64)
             st["h_scales"] = graph.tile([P, NODES], U8, name="h_scales", align_bytes=64)
             st["stats"] = graph.tile([P, BLOCKS, 6], F32, name="stats")
-            st["twice_mean"] = graph.tile([P, BLOCKS], F32, name="twice_mean")
-            st["gap"] = graph.tile([P, BLOCKS], F32, name="gap")
-            st["sumsq"] = graph.tile([P, BLOCKS], F32, name="sumsq")
+            st["mean_var"] = graph.tile([P, BLOCKS, 2], F32, name="mean_var")
+            st["mean"] = st["mean_var"][:, :, 0]
             st["inv_norm"] = graph.tile([P, BLOCKS], F32, name="inv_norm")
-            st["norm"] = graph.tile([P, BLOCKS], F32, name="norm")
+            st["norm"] = graph.tile([P, BLOCKS], F32, name="norm")[:]
             st["mean_bc"] = graph.tile([P, NODES], F32, name="mean_bc")
             st["inv_root"] = graph.tile([P, TRI], F32, name="inv_root")
             st["inv_denom"] = graph.tile([P, TRI], F32, name="inv_denom")
@@ -151,26 +150,16 @@ def tile_pearsonattention_pa_kernel(tc, h, W_h, beta, out):
         def node_stats(b, r):
             nc.vector.bn_stats(out=state[b]["stats"][:, r, :], in_=state[b]["wh", r][:])
 
-        def mean(b):
-            stats = state[b]["stats"]
-            nc.vector.tensor_tensor(
-                out=state[b]["twice_mean"][:], in0=stats[:, :, 1], in1=stats[:, :, 4], op=ALU.add
-            )
+        def mean_and_variance(b, r):
+            nc.vector.bn_aggr(out=state[b]["mean_var"][:, r, :], in_=state[b]["stats"][:, r, :])
 
         def norm(b):
             st = state[b]
-            stats, gap, sumsq = st["stats"], st["gap"], st["sumsq"]
-            nc.gpsimd.tensor_tensor(out=gap[:], in0=stats[:, :, 1], in1=stats[:, :, 4], op=ALU.subtract)
-            nc.gpsimd.tensor_tensor(out=sumsq[:], in0=stats[:, :, 2], in1=stats[:, :, 5], op=ALU.add)
-            nc.gpsimd.tensor_tensor(out=gap[:], in0=gap[:], in1=gap[:], op=ALU.mult)
-            nc.gpsimd.tensor_scalar(
-                out=gap[:], in0=gap[:], scalar1=float(FEATS // 4), scalar2=0.0, op0=ALU.mult, op1=ALU.add
-            )
-            nc.gpsimd.tensor_tensor(out=sumsq[:], in0=sumsq[:], in1=gap[:], op=ALU.add)
+            var = st["mean_var"][:, :, 1]
             nc.scalar.activation(
-                out=st["inv_norm"][:], in_=sumsq[:], func=ACT.Abs_reciprocal_sqrt, bias=tiny_col[:]
+                out=st["inv_norm"][:], in_=var, func=ACT.Abs_reciprocal_sqrt, scale=1.0 / FEATS, bias=tiny_col[:]
             )
-            nc.gpsimd.tensor_tensor(out=st["norm"][:], in0=sumsq[:], in1=st["inv_norm"][:], op=ALU.mult)
+            nc.gpsimd.tensor_tensor(out=st["norm"], in0=var, in1=st["inv_norm"][:], op=ALU.mult)
 
         def spread(b, what):
             bank = ps_bc.tile([P, NODES], F32, name="spread_" + what)
@@ -181,9 +170,7 @@ def tile_pearsonattention_pa_kernel(tc, h, W_h, beta, out):
             state[b]["spread_" + what] = bank
 
         def copy_mean(b):
-            nc.scalar.activation(
-                out=state[b]["mean_bc"][:], in_=state[b]["spread_twice_mean"][:], func=ACT.Copy, scale=0.5
-            )
+            nc.scalar.copy(out=state[b]["mean_bc"][:], in_=state[b]["spread_mean"][:])
 
         def inverse_root(b):
             st = state[b]
@@ -289,83 +276,82 @@ def tile_pearsonattention_pa_kernel(tc, h, W_h, beta, out):
 
         with tc.manual_schedule():
             for s in range(-3, GRAPHS + 3):
-                if live(s - 1):
-                    inverse_denominator(s - 1)
+                behind, ahead = s - 1, s + 1
+                if live(behind):
+                    inverse_denominator(behind)
                 if live(s - 3):
                     for c in range(1, BLOCKS):
                         copy_mirror(s - 3, c)
-                if live(s):
-                    copy_mean(s)
-                    inverse_root(s)
-                if live(s + 3) and s + 3 != 1:
+                if live(s + 3):
                     for half in range(2):
                         transpose_h(s + 3, half)
-                    for half in range(2):
-                        group_h(s + 3, half)
                 if live(s):
-                    if s < GRAPHS - 1:
+                    if live(ahead):
                         project_t(s, 2)
                     project_t(s, 3)
+                    copy_mean(s)
+                    inverse_root(s)
+                if live(behind):
+                    for i in range(len(BANKS)):
+                        absolute(behind, i)
                 if live(s - 2):
                     for c in range(1, BLOCKS):
                         mirror(s - 2, c)
+                if live(s + 3) and s < 0:
+                    for half in range(2):
+                        group_h(s + 3, half)
                 if live(s):
                     centre(s, 0)
-                    if live(s + 1):
-                        mean(s + 1)
+                    if live(ahead):
+                        mean_and_variance(ahead, 3)
                     for r in range(1, BLOCKS):
                         centre(s, r)
                 if live(s + 2):
                     quantise_h(s + 2, 0)
-                    if s == -1:
-                        mean(0)
+                    if live(ahead) and not live(s):
+                        mean_and_variance(ahead, 3)
                     quantise_h(s + 2, 1)
-                if live(s + 1):
-                    spread(s + 1, "twice_mean")
-                if live(s - 1):
-                    for i in range(len(BANKS)):
-                        absolute(s - 1, i)
-                if live(s + 1):
-                    norm(s + 1)
+                if live(ahead):
+                    norm(ahead)
+                    if live(s):
+                        spread(ahead, "mean")
+                        spread(ahead, "norm")
                 if live(s + 2):
                     for r in range(3):
                         project(s + 2, r)
-                    if s + 3 == 1:
-                        for half in range(2):
-                            transpose_h(1, half)
-                        for half in range(2):
-                            group_h(1, half)
-                    if live(s + 1):
-                        spread(s + 1, "norm")
+                    if live(ahead) and not live(s):
+                        spread(ahead, "mean")
+                        spread(ahead, "norm")
                     if live(s):
                         quantise_x(s)
                         for i in range(len(BANKS)):
                             covariance(s, i)
-                    node_stats(s + 2, 0)
-                    project(s + 2, 3)
-                    node_stats(s + 2, 1)
-                    if live(s + 1):
-                        project_t(s + 1, 0)
-                    node_stats(s + 2, 2)
-                    if live(s + 1):
-                        project_t(s + 1, 1)
-                    node_stats(s + 2, 3)
-                    if live(s - 1):
+                    for r in range(BLOCKS):
+                        node_stats(s + 2, r)
+                        if r == 0:
+                            project(s + 2, 3)
+                        else:
+                            mean_and_variance(s + 2, r - 1)
+                            if live(ahead) and r < 3:
+                                project_t(ahead, r - 1)
+                    if live(behind):
                         for r in (0, 1, 3, 2):
-                            scale(s - 1, r)
-                        store(s - 1, 0)
+                            scale(behind, r)
+                        store(behind, 0)
                 else:
-                    if live(s + 1):
+                    if live(ahead):
                         for r in range(3):
-                            project_t(s + 1, r)
-                        spread(s + 1, "norm")
-                    if live(s - 1):
-                        scale(s - 1, 0)
-                        store(s - 1, 0)
+                            project_t(ahead, r)
+                    if live(behind):
+                        scale(behind, 0)
+                        store(behind, 0)
                     if live(s):
                         quantise_x(s)
                         for i in range(len(BANKS)):
                             covariance(s, i)
-                    if live(s - 1):
+                    if live(behind):
                         for r in (1, 3, 2):
-                            scale(s - 1, r)
+                            scale(behind, r)
+                if live(s + 3) and s >= 0:
+                    for half in range(2):
+                        group_h(s + 3, half)

@@ -19,7 +19,6 @@ FEATS_IN = 512
 FEATS = 512
 BLOCKS = NODES // P
 HALF = NODES // 2
-W_SPLIT = 80
 EPS = 1e-8
 TINY = 1e-30
 
@@ -37,9 +36,8 @@ def tile_pearsonattention_pa_kernel(tc, h, W_h, beta, out):
         const = ctx.enter_context(tc.tile_pool(name="const", bufs=1))
         halves = ctx.enter_context(tc.tile_pool(name="halves", bufs=2 * GRAPHS))
         graph = ctx.enter_context(tc.tile_pool(name="graph", bufs=GRAPHS))
-        ps_v = ctx.enter_context(tc.psum_pool(name="ps_v", bufs=3))
-        ps_s = ctx.enter_context(tc.psum_pool(name="ps_s", bufs=3))
-        ps_bc = ctx.enter_context(tc.psum_pool(name="ps_bc", bufs=1))
+        ps_v = ctx.enter_context(tc.psum_pool(name="ps_v", bufs=4))
+        ps_s = ctx.enter_context(tc.psum_pool(name="ps_s", bufs=4))
 
         w_raw = const.tile([P, PACK, FEATS], BF16)
         nc.sync.dma_start(
@@ -72,8 +70,7 @@ def tile_pearsonattention_pa_kernel(tc, h, W_h, beta, out):
         w_grp = const.tile([P, FEATS, PACK], BF16, align_bytes=64)
         w_to = w_grp[:].rearrange("p (tg pg) t -> p tg pg t", tg=PACK)
         w_from = w_raw[:].rearrange("p t (pg tg) -> p tg pg t", tg=PACK)
-        nc.vector.tensor_copy(out=w_to[:, :, 0:W_SPLIT, :], in_=w_from[:, :, 0:W_SPLIT, :])
-        nc.scalar.copy(out=w_to[:, :, W_SPLIT:, :], in_=w_from[:, :, W_SPLIT:, :])
+        nc.vector.tensor_copy(out=w_to, in_=w_from)
         w_codes = const.tile([P, FEATS], U32, align_bytes=64)
         w_scales = const.tile([P, FEATS], U8, align_bytes=64)
         nc.vector.quantize_mx(
@@ -153,16 +150,23 @@ def tile_pearsonattention_pa_kernel(tc, h, W_h, beta, out):
         def mean_and_variance(b, r):
             nc.vector.bn_aggr(out=state[b]["mean_var"][:, r, :], in_=state[b]["stats"][:, r, :])
 
+        def inverse_norm(b):
+            nc.scalar.activation(
+                out=state[b]["inv_norm"][:],
+                in_=state[b]["mean_var"][:, :, 1],
+                func=ACT.Abs_reciprocal_sqrt,
+                scale=1.0 / FEATS,
+                bias=tiny_col[:],
+            )
+
         def norm(b):
             st = state[b]
-            var = st["mean_var"][:, :, 1]
-            nc.scalar.activation(
-                out=st["inv_norm"][:], in_=var, func=ACT.Abs_reciprocal_sqrt, scale=1.0 / FEATS, bias=tiny_col[:]
+            nc.vector.tensor_tensor(
+                out=st["norm"], in0=st["mean_var"][:, :, 1], in1=st["inv_norm"][:], op=ALU.mult
             )
-            nc.gpsimd.tensor_tensor(out=st["norm"], in0=var, in1=st["inv_norm"][:], op=ALU.mult)
 
         def spread(b, what):
-            bank = ps_bc.tile([P, NODES], F32, name="spread_" + what)
+            bank = ps_s.tile([P, NODES], F32, tag="s")
             for r in range(BLOCKS):
                 nc.tensor.transpose(
                     bank[:, block(r)], state[b][what][:, r : r + 1].to_broadcast([P, P]), ident[:]
@@ -253,9 +257,10 @@ def tile_pearsonattention_pa_kernel(tc, h, W_h, beta, out):
                 op0=ALU.mult,
                 op1=ALU.mult,
             )
+            store(b, r, slice(r * P, NODES))
 
-        def store(b, r):
-            nc.sync.dma_start(out=out[b, r * P : (r + 1) * P, :], in_=state[b]["result"][:, r, :])
+        def store(b, r, cols):
+            nc.sync.dma_start(out=out[b, r * P : (r + 1) * P, cols], in_=state[b]["result"][:, r, cols])
 
         def mirror(b, c):
             bank = ps_s.tile([P, c * P], F32, tag="s")
@@ -269,7 +274,7 @@ def tile_pearsonattention_pa_kernel(tc, h, W_h, beta, out):
                 nc.vector.tensor_copy(out=out_cols, in_=state[b]["mirror", c][:])
             else:
                 nc.scalar.copy(out=out_cols, in_=state[b]["mirror", c][:])
-            store(b, c)
+            store(b, c, slice(0, c * P))
 
         def live(b):
             return 0 <= b < GRAPHS
@@ -277,29 +282,25 @@ def tile_pearsonattention_pa_kernel(tc, h, W_h, beta, out):
         with tc.manual_schedule():
             for s in range(-3, GRAPHS + 3):
                 behind, ahead = s - 1, s + 1
-                if live(behind):
-                    inverse_denominator(behind)
                 if live(s - 3):
                     for c in range(1, BLOCKS):
                         copy_mirror(s - 3, c)
-                if live(s + 3):
-                    for half in range(2):
-                        transpose_h(s + 3, half)
+                if live(behind):
+                    inverse_denominator(behind)
                 if live(s):
                     if live(ahead):
                         project_t(s, 2)
                     project_t(s, 3)
                     copy_mean(s)
-                    inverse_root(s)
                 if live(behind):
                     for i in range(len(BANKS)):
                         absolute(behind, i)
+                if live(s + 3):
+                    for half in range(2):
+                        transpose_h(s + 3, half)
                 if live(s - 2):
                     for c in range(1, BLOCKS):
                         mirror(s - 2, c)
-                if live(s + 3) and s < 0:
-                    for half in range(2):
-                        group_h(s + 3, half)
                 if live(s):
                     centre(s, 0)
                     if live(ahead):
@@ -311,21 +312,26 @@ def tile_pearsonattention_pa_kernel(tc, h, W_h, beta, out):
                     if live(ahead) and not live(s):
                         mean_and_variance(ahead, 3)
                     quantise_h(s + 2, 1)
+                if live(s):
+                    inverse_root(s)
                 if live(ahead):
-                    norm(ahead)
                     if live(s):
                         spread(ahead, "mean")
-                        spread(ahead, "norm")
+                    inverse_norm(ahead)
                 if live(s + 2):
                     for r in range(3):
                         project(s + 2, r)
                     if live(ahead) and not live(s):
                         spread(ahead, "mean")
-                        spread(ahead, "norm")
                     if live(s):
                         quantise_x(s)
                         for i in range(len(BANKS)):
                             covariance(s, i)
+                    if live(s + 3) and live(s):
+                        for half in range(2):
+                            group_h(s + 3, half)
+                    if live(ahead):
+                        norm(ahead)
                     for r in range(BLOCKS):
                         node_stats(s + 2, r)
                         if r == 0:
@@ -337,21 +343,23 @@ def tile_pearsonattention_pa_kernel(tc, h, W_h, beta, out):
                     if live(behind):
                         for r in (0, 1, 3, 2):
                             scale(behind, r)
-                        store(behind, 0)
                 else:
                     if live(ahead):
                         for r in range(3):
                             project_t(ahead, r)
                     if live(behind):
                         scale(behind, 0)
-                        store(behind, 0)
                     if live(s):
                         quantise_x(s)
                         for i in range(len(BANKS)):
                             covariance(s, i)
+                    if live(ahead):
+                        norm(ahead)
                     if live(behind):
                         for r in (1, 3, 2):
                             scale(behind, r)
-                if live(s + 3) and s >= 0:
+                if live(s + 3) and not live(s):
                     for half in range(2):
                         group_h(s + 3, half)
+                if live(ahead):
+                    spread(ahead, "norm")

@@ -22,10 +22,8 @@ HALF = NODES // 2
 EPS = 1e-8
 TINY = 1e-30
 
-BANKS = ((0,), (1, 3), (2,))
-FIRST = {0: 0, 1: 512, 3: 896, 2: 1024}
-TRI = 1280
-MOVING = {0: ((0, 512),), 1: ((128, 384), (384, 512)), 2: ((256, 512),), 3: ((384, 512),)}
+MX_WIDTHS = (128, 256, 512)
+TURNED = 0
 
 FLOPS = 2 * GRAPHS * NODES * FEATS_IN * FEATS + 2 * GRAPHS * NODES * NODES * FEATS
 
@@ -91,20 +89,19 @@ def tile_pearsonattention_pa_kernel(tc, h, W_h, beta, out):
             st["inv_norm"] = graph.tile([P, BLOCKS], F32, name="inv_norm")
             st["norm"] = graph.tile([P, BLOCKS], F32, name="norm")[:]
             st["mean_bc"] = graph.tile([P, NODES], F32, name="mean_bc")
-            st["inv_root"] = graph.tile([P, TRI], F32, name="inv_root")
-            st["inv_denom"] = graph.tile([P, TRI], F32, name="inv_denom")
+            st["inv_root"] = graph.tile([P, BLOCKS, NODES], F32, name="inv_root")
+            st["inv_denom"] = graph.tile([P, BLOCKS, NODES], F32, name="inv_denom")
             st["x_grp"] = graph.tile([P, NODES, PACK], BF16, name="x_grp", align_bytes=64)
             st["x_codes"] = graph.tile([P, NODES], U32, name="x_codes", align_bytes=64)
             st["x_scales"] = graph.tile([P, NODES], U8, name="x_scales", align_bytes=64)
-            st["magnitude"] = graph.tile([P, TRI], F32, name="magnitude")
             st["result"] = graph.tile([P, BLOCKS, NODES], F32, name="result")
             state.append(st)
 
         def block(r):
             return slice(r * P, (r + 1) * P)
 
-        def tri(r):
-            return slice(FIRST[r], FIRST[r] + NODES - r * P)
+        def upper(r):
+            return slice(r * P, NODES)
 
         def transpose_h(b, half):
             words = h_raw[2 * b + half][:].bitcast(F32).rearrange("p (j u w) -> p j u w", j=2, u=2)
@@ -180,15 +177,19 @@ def tile_pearsonattention_pa_kernel(tc, h, W_h, beta, out):
             st = state[b]
             for r in range(BLOCKS):
                 nc.scalar.activation(
-                    out=st["inv_root"][:, tri(r)],
-                    in_=st["spread_norm"][:, r * P :],
+                    out=st["inv_root"][:, r, upper(r)],
+                    in_=st["spread_norm"][:, upper(r)],
                     func=ACT.Abs_reciprocal_sqrt,
                     scale=st["norm"][:, r : r + 1],
                     bias=eps_col[:],
                 )
 
         def inverse_denominator(b):
-            nc.scalar.activation(out=state[b]["inv_denom"][:], in_=state[b]["inv_root"][:], func=ACT.Square)
+            st = state[b]
+            for r in range(BLOCKS):
+                nc.scalar.activation(
+                    out=st["inv_denom"][:, r, upper(r)], in_=st["inv_root"][:, r, upper(r)], func=ACT.Square
+                )
 
         def project_t(b, r):
             st = state[b]
@@ -222,38 +223,60 @@ def tile_pearsonattention_pa_kernel(tc, h, W_h, beta, out):
                 in_=st["x_grp"][:].rearrange("p n t -> p (n t)"),
             )
 
-        def covariance(b, i):
-            st = state[b]
-            start = FIRST[BANKS[i][0]]
-            cov = ps_s.tile([P, sum([NODES - r * P for r in BANKS[i]])], F32, tag="s")
-            for r in BANKS[i]:
-                for m0, m1 in MOVING[r]:
-                    at = FIRST[r] - start + m0 - r * P
-                    nc.tensor.matmul_mx(
-                        out=cov[:, at : at + m1 - m0],
-                        lhsT=st["x_codes"][:, block(r)].bitcast(FP8X4),
-                        lhsT_scale=st["x_scales"][:, block(r)],
-                        rhs=st["x_codes"][:, m0:m1].bitcast(FP8X4),
-                        rhs_scale=st["x_scales"][:, m0:m1],
-                        start=True,
-                        stop=True,
-                    )
-            st["cov", i] = cov
+        x_node = const.tile([P, BLOCKS, FEATS], BF16)
 
-        def absolute(b, i):
-            start = FIRST[BANKS[i][0]]
-            width = sum([NODES - r * P for r in BANKS[i]])
+        def centre_node(b, r):
             nc.scalar.activation(
-                out=state[b]["magnitude"][:, start : start + width], in_=state[b]["cov", i][:], func=ACT.Abs
+                out=x_node[:, r, :],
+                in_=state[b]["wh", r][:],
+                func=ACT.Identity,
+                scale=-1.0,
+                bias=state[b]["mean_var"][:, r, 0:1],
+            )
+
+        def turn_x(b, half):
+            x_t = ps_s.tile([P, 2, 2, P], F32, tag="s")
+            for j in range(2):
+                words = x_node[:, 2 * half + j, :].bitcast(F32)
+                for u in range(2):
+                    nc.tensor.transpose(x_t[:, j, u, :], words[:, block(u)], ident[:])
+            state[b]["x_t", half] = x_t
+
+        def group_x(b, half):
+            x_words = state[b]["x_grp"][:].rearrange("p n t -> p (n t)").bitcast(F32)
+            copy = nc.scalar.copy if half == 0 else nc.vector.tensor_copy
+            copy(
+                out=x_words.rearrange("p (r n u) -> p r n u", r=BLOCKS, u=2)[:, 2 * half : 2 * half + 2, :, :],
+                in_=state[b]["x_t", half][:].rearrange("p j u n -> p j n u"),
+            )
+
+        def covariance(b, r):
+            st = state[b]
+            width = min([n for n in MX_WIDTHS if n >= NODES - r * P])
+            cov = ps_s.tile([P, width], F32, tag="s")
+            nc.tensor.matmul_mx(
+                out=cov[:],
+                lhsT=st["x_codes"][:, block(r)].bitcast(FP8X4),
+                lhsT_scale=st["x_scales"][:, block(r)],
+                rhs=st["x_codes"][:, NODES - width :].bitcast(FP8X4),
+                rhs_scale=st["x_scales"][:, NODES - width :],
+                start=True,
+                stop=True,
+            )
+            st["cov", r] = cov[:, width - NODES + r * P :]
+
+        def absolute(b, r):
+            nc.scalar.activation(
+                out=state[b]["result"][:, r, upper(r)], in_=state[b]["cov", r], func=ACT.Abs
             )
 
         def scale(b, r):
             st = state[b]
             nc.vector.scalar_tensor_tensor(
-                out=st["result"][:, r, r * P :],
-                in0=st["magnitude"][:, tri(r)],
+                out=st["result"][:, r, upper(r)],
+                in0=st["result"][:, r, upper(r)],
                 scalar=beta_col[:, 0:1],
-                in1=st["inv_denom"][:, tri(r)],
+                in1=st["inv_denom"][:, r, upper(r)],
                 op0=ALU.mult,
                 op1=ALU.mult,
             )
@@ -282,26 +305,26 @@ def tile_pearsonattention_pa_kernel(tc, h, W_h, beta, out):
         with tc.manual_schedule():
             for s in range(-3, GRAPHS + 3):
                 behind, ahead = s - 1, s + 1
+                if live(s + 3) and s < 0:
+                    for half in range(2):
+                        transpose_h(s + 3, half)
                 if live(s - 3):
                     for c in range(1, BLOCKS):
                         copy_mirror(s - 3, c)
-                if live(behind):
-                    inverse_denominator(behind)
-                if live(s):
+                if live(s) and s != TURNED:
+                    copy_mean(s)
                     if live(ahead):
                         project_t(s, 2)
                     project_t(s, 3)
-                    copy_mean(s)
                 if live(behind):
-                    for i in range(len(BANKS)):
-                        absolute(behind, i)
-                if live(s + 3):
+                    inverse_denominator(behind)
+                if live(s + 3) and s >= 0:
                     for half in range(2):
                         transpose_h(s + 3, half)
-                if live(s - 2):
-                    for c in range(1, BLOCKS):
-                        mirror(s - 2, c)
-                if live(s):
+                if live(behind):
+                    for r in range(BLOCKS):
+                        absolute(behind, r)
+                if live(s) and s != TURNED:
                     centre(s, 0)
                     if live(ahead):
                         mean_and_variance(ahead, 3)
@@ -309,57 +332,72 @@ def tile_pearsonattention_pa_kernel(tc, h, W_h, beta, out):
                         centre(s, r)
                 if live(s + 2):
                     quantise_h(s + 2, 0)
-                    if live(ahead) and not live(s):
+                    if live(ahead) and not (live(s) and s != TURNED):
                         mean_and_variance(ahead, 3)
                     quantise_h(s + 2, 1)
+                if live(s - 2):
+                    for c in range(1, BLOCKS):
+                        mirror(s - 2, c)
+                if live(ahead) and ahead != TURNED:
+                    spread(ahead, "mean")
                 if live(s):
                     inverse_root(s)
-                if live(ahead):
-                    if live(s):
-                        spread(ahead, "mean")
-                    inverse_norm(ahead)
                 if live(s + 2):
                     for r in range(3):
                         project(s + 2, r)
-                    if live(ahead) and not live(s):
-                        spread(ahead, "mean")
+                    if ahead == TURNED:
+                        centre_node(ahead, 3)
+                    if live(ahead):
+                        inverse_norm(ahead)
                     if live(s):
                         quantise_x(s)
-                        for i in range(len(BANKS)):
-                            covariance(s, i)
-                    if live(s + 3) and live(s):
+                        for r in range(BLOCKS):
+                            covariance(s, r)
+                    if live(s + 3):
                         for half in range(2):
                             group_h(s + 3, half)
-                    if live(ahead):
-                        norm(ahead)
                     for r in range(BLOCKS):
                         node_stats(s + 2, r)
                         if r == 0:
                             project(s + 2, 3)
-                        else:
-                            mean_and_variance(s + 2, r - 1)
-                            if live(ahead) and r < 3:
-                                project_t(ahead, r - 1)
+                            continue
+                        mean_and_variance(s + 2, r - 1)
+                        if s + 2 == TURNED:
+                            centre_node(s + 2, r - 1)
+                        if live(ahead) and ahead != TURNED and r < 3:
+                            project_t(ahead, r - 1)
+                        if r == 1 and live(ahead):
+                            norm(ahead)
+                            if ahead == TURNED:
+                                for half in range(2):
+                                    turn_x(ahead, half)
+                    if live(ahead):
+                        spread(ahead, "norm")
                     if live(behind):
-                        for r in (0, 1, 3, 2):
+                        scale(behind, 0)
+                    if ahead == TURNED:
+                        for half in range(2):
+                            group_x(ahead, half)
+                    if live(behind):
+                        for r in range(1, BLOCKS):
                             scale(behind, r)
                 else:
                     if live(ahead):
                         for r in range(3):
                             project_t(ahead, r)
+                        inverse_norm(ahead)
                     if live(behind):
                         scale(behind, 0)
                     if live(s):
                         quantise_x(s)
-                        for i in range(len(BANKS)):
-                            covariance(s, i)
+                        for r in range(BLOCKS):
+                            covariance(s, r)
                     if live(ahead):
                         norm(ahead)
+                        spread(ahead, "norm")
                     if live(behind):
-                        for r in (1, 3, 2):
+                        for r in range(1, BLOCKS):
                             scale(behind, r)
-                if live(s + 3) and not live(s):
-                    for half in range(2):
-                        group_h(s + 3, half)
-                if live(ahead):
-                    spread(ahead, "norm")
+                    if live(s + 3):
+                        for half in range(2):
+                            group_h(s + 3, half)

@@ -302,7 +302,7 @@ def tile_pearsonattention_pa_kernel(tc, h, W_h, beta, out):
         def live(b):
             return 0 <= b < GRAPHS
 
-        with tc.manual_schedule():
+        with tc.manual_schedule(engines={mybir.EngineType.DVE, mybir.EngineType.Activation}):
             for s in range(-3, GRAPHS + 3):
                 behind, ahead = s - 1, s + 1
                 if live(s + 3) and s < 0:

from contextlib import ExitStack

import concourse.mybir as mybir
from concourse.masks import make_identity

F32 = mybir.dt.float32
BF16 = mybir.dt.bfloat16
U32 = mybir.dt.uint32
U8 = mybir.dt.uint8
FP8X4 = mybir.dt.float8_e4m3fn_x4
ACT = mybir.ActivationFunctionType
ALU = mybir.AluOpType

P = 128
PACK = 4
GRAPHS = 4
NODES = 512
FEATS_IN = 512
FEATS = 512
BLOCKS = NODES // P
HALF = NODES // 2
EPS = 1e-8
TINY = 1e-30

MX_WIDTHS = (128, 256, 512)
TURNED = 0

FLOPS = 2 * GRAPHS * NODES * FEATS_IN * FEATS + 2 * GRAPHS * NODES * NODES * FEATS


def tile_pearsonattention_pa_kernel(tc, h, W_h, beta, out):
    nc = tc.nc
    with ExitStack() as ctx:
        const = ctx.enter_context(tc.tile_pool(name="const", bufs=1))
        halves = ctx.enter_context(tc.tile_pool(name="halves", bufs=2 * GRAPHS))
        graph = ctx.enter_context(tc.tile_pool(name="graph", bufs=GRAPHS))
        ps_v = ctx.enter_context(tc.psum_pool(name="ps_v", bufs=4))
        ps_s = ctx.enter_context(tc.psum_pool(name="ps_s", bufs=4))

        w_raw = const.tile([P, PACK, FEATS], BF16)
        nc.sync.dma_start(
            out=w_raw[:].rearrange("p (u e) g -> p u e g", u=2),
            in_=W_h.rearrange("(u p e) g -> p u e g", u=2, e=2),
        )
        beta_bf = const.tile([P, 1], BF16)
        nc.scalar.dma_start(out=beta_bf[:], in_=beta.partition_broadcast(P))
        h_raw = []
        for b in range(GRAPHS):
            for half in range(2):
                raw = halves.tile([P, 2 * FEATS_IN], BF16, name="h_raw")
                nc.sync.dma_start(
                    out=raw[:].rearrange("p (j k) -> p j k", j=2),
                    in_=h[b, half * HALF : (half + 1) * HALF, :].rearrange("(j p) k -> p j k", p=P),
                )
                h_raw.append(raw)

        ident = const.tile([P, P], F32)
        make_identity(nc, ident[:])
        eps_col = const.tile([P, 1], F32)
        nc.vector.memset(eps_col[:], EPS)
        tiny_col = const.tile([P, 1], F32)
        nc.vector.memset(tiny_col[:], TINY)
        beta_col = const.tile([P, 1], F32)
        nc.gpsimd.tensor_copy(out=beta_col[:], in_=beta_bf[:])
        warm = const.tile([P, 1], F32)
        nc.scalar.activation(out=warm[:], in_=eps_col[:], func=ACT.Abs_reciprocal_sqrt)

        w_grp = const.tile([P, FEATS, PACK], BF16, align_bytes=64)
        w_to = w_grp[:].rearrange("p (tg pg) t -> p tg pg t", tg=PACK)
        w_from = w_raw[:].rearrange("p t (pg tg) -> p tg pg t", tg=PACK)
        nc.vector.tensor_copy(out=w_to, in_=w_from)
        w_codes = const.tile([P, FEATS], U32, align_bytes=64)
        w_scales = const.tile([P, FEATS], U8, align_bytes=64)
        nc.vector.quantize_mx(
            out=w_codes[:].bitcast(FP8X4),
            scales=w_scales[:],
            in_=w_grp[:].rearrange("p c t -> p (c t)"),
        )

        state = []
        for b in range(GRAPHS):
            st = dict()
            st["h_grp"] = graph.tile([P, NODES * PACK], BF16, name="h_grp", align_bytes=64)
            st["h_codes"] = graph.tile([P, NODES], U32, name="h_codes", align_bytes=64)
            st["h_scales"] = graph.tile([P, NODES], U8, name="h_scales", align_bytes=64)
            st["stats"] = graph.tile([P, BLOCKS, 6], F32, name="stats")
            st["mean_var"] = graph.tile([P, BLOCKS, 2], F32, name="mean_var")
            st["mean"] = st["mean_var"][:, :, 0]
            st["inv_norm"] = graph.tile([P, BLOCKS], F32, name="inv_norm")
            st["norm"] = graph.tile([P, BLOCKS], F32, name="norm")[:]
            st["mean_bc"] = graph.tile([P, NODES], F32, name="mean_bc")
            st["inv_root"] = graph.tile([P, BLOCKS, NODES], F32, name="inv_root")
            st["inv_denom"] = graph.tile([P, BLOCKS, NODES], F32, name="inv_denom")
            st["x_grp"] = graph.tile([P, NODES, PACK], BF16, name="x_grp", align_bytes=64)
            st["x_codes"] = graph.tile([P, NODES], U32, name="x_codes", align_bytes=64)
            st["x_scales"] = graph.tile([P, NODES], U8, name="x_scales", align_bytes=64)
            st["result"] = graph.tile([P, BLOCKS, NODES], F32, name="result")
            state.append(st)

        def block(r):
            return slice(r * P, (r + 1) * P)

        def upper(r):
            return slice(r * P, NODES)

        def transpose_h(b, half):
            words = h_raw[2 * b + half][:].bitcast(F32).rearrange("p (j u w) -> p j u w", j=2, u=2)
            h_t = ps_s.tile([P, 2, 2, P], F32, tag="s")
            for j in range(2):
                for u in range(2):
                    nc.tensor.transpose(h_t[:, j, u, :], words[:, j, u, :], ident[:])
            state[b]["h_t", half] = h_t

        def group_h(b, half):
            grp_words = state[b]["h_grp"][:].bitcast(F32).rearrange("p (r n u) -> p r n u", r=BLOCKS, u=2)
            nc.scalar.copy(
                out=grp_words[:, 2 * half : 2 * half + 2, :, :],
                in_=state[b]["h_t", half][:].rearrange("p j u n -> p j n u"),
            )

        def quantise_h(b, half):
            st = state[b]
            cols = slice(half * HALF, (half + 1) * HALF)
            nc.vector.quantize_mx(
                out=st["h_codes"][:, cols].bitcast(FP8X4),
                scales=st["h_scales"][:, cols],
                in_=st["h_grp"][:, half * HALF * PACK : (half + 1) * HALF * PACK],
            )

        def project(b, r):
            st = state[b]
            wh = ps_v.tile([P, FEATS], F32, tag="v")
            nc.tensor.matmul_mx(
                out=wh[:],
                lhsT=st["h_codes"][:, block(r)].bitcast(FP8X4),
                lhsT_scale=st["h_scales"][:, block(r)],
                rhs=w_codes[:].bitcast(FP8X4),
                rhs_scale=w_scales[:],
                start=True,
                stop=True,
            )
            st["wh", r] = wh

        def node_stats(b, r):
            nc.vector.bn_stats(out=state[b]["stats"][:, r, :], in_=state[b]["wh", r][:])

        def mean_and_variance(b, r):
            nc.vector.bn_aggr(out=state[b]["mean_var"][:, r, :], in_=state[b]["stats"][:, r, :])

        def inverse_norm(b):
            nc.scalar.activation(
                out=state[b]["inv_norm"][:],
                in_=state[b]["mean_var"][:, :, 1],
                func=ACT.Abs_reciprocal_sqrt,
                scale=1.0 / FEATS,
                bias=tiny_col[:],
            )

        def norm(b):
            st = state[b]
            nc.vector.tensor_tensor(
                out=st["norm"], in0=st["mean_var"][:, :, 1], in1=st["inv_norm"][:], op=ALU.mult
            )

        def spread(b, what):
            bank = ps_s.tile([P, NODES], F32, tag="s")
            for r in range(BLOCKS):
                nc.tensor.transpose(
                    bank[:, block(r)], state[b][what][:, r : r + 1].to_broadcast([P, P]), ident[:]
                )
            state[b]["spread_" + what] = bank

        def copy_mean(b):
            nc.scalar.copy(out=state[b]["mean_bc"][:], in_=state[b]["spread_mean"][:])

        def inverse_root(b):
            st = state[b]
            for r in range(BLOCKS):
                nc.scalar.activation(
                    out=st["inv_root"][:, r, upper(r)],
                    in_=st["spread_norm"][:, upper(r)],
                    func=ACT.Abs_reciprocal_sqrt,
                    scale=st["norm"][:, r : r + 1],
                    bias=eps_col[:],
                )

        def inverse_denominator(b):
            st = state[b]
            for r in range(BLOCKS):
                nc.scalar.activation(
                    out=st["inv_denom"][:, r, upper(r)], in_=st["inv_root"][:, r, upper(r)], func=ACT.Square
                )

        def project_t(b, r):
            st = state[b]
            wh_t = ps_v.tile([P, PACK, P], F32, tag="v")
            for tg in range(PACK):
                nc.tensor.matmul_mx(
                    out=wh_t[:, tg, :],
                    lhsT=w_codes[:, block(tg)].bitcast(FP8X4),
                    lhsT_scale=w_scales[:, block(tg)],
                    rhs=st["h_codes"][:, block(r)].bitcast(FP8X4),
                    rhs_scale=st["h_scales"][:, block(r)],
                    start=True,
                    stop=True,
                )
            st["wh_t", r] = wh_t

        def centre(b, r):
            st = state[b]
            nc.vector.tensor_tensor(
                out=st["x_grp"][:, block(r), :],
                in0=st["wh_t", r][:].rearrange("p t n -> p n t"),
                in1=st["mean_bc"][:, block(r)].unsqueeze(2).to_broadcast([P, P, PACK]),
                op=ALU.subtract,
            )

        def quantise_x(b):
            st = state[b]
            nc.vector.quantize_mx(
                out=st["x_codes"][:].bitcast(FP8X4),
                scales=st["x_scales"][:],
                in_=st["x_grp"][:].rearrange("p n t -> p (n t)"),
            )

        x_node = const.tile([P, BLOCKS, FEATS], BF16)

        def centre_node(b, r):
            nc.scalar.activation(
                out=x_node[:, r, :],
                in_=state[b]["wh", r][:],
                func=ACT.Identity,
                scale=-1.0,
                bias=state[b]["mean_var"][:, r, 0:1],
            )

        def turn_x(b, half):
            x_t = ps_s.tile([P, 2, 2, P], F32, tag="s")
            for j in range(2):
                words = x_node[:, 2 * half + j, :].bitcast(F32)
                for u in range(2):
                    nc.tensor.transpose(x_t[:, j, u, :], words[:, block(u)], ident[:])
            state[b]["x_t", half] = x_t

        def group_x(b, half):
            x_words = state[b]["x_grp"][:].rearrange("p n t -> p (n t)").bitcast(F32)
            copy = nc.scalar.copy if half == 0 else nc.vector.tensor_copy
            copy(
                out=x_words.rearrange("p (r n u) -> p r n u", r=BLOCKS, u=2)[:, 2 * half : 2 * half + 2, :, :],
                in_=state[b]["x_t", half][:].rearrange("p j u n -> p j n u"),
            )

        def covariance(b, r):
            st = state[b]
            width = min([n for n in MX_WIDTHS if n >= NODES - r * P])
            cov = ps_s.tile([P, width], F32, tag="s")
            nc.tensor.matmul_mx(
                out=cov[:],
                lhsT=st["x_codes"][:, block(r)].bitcast(FP8X4),
                lhsT_scale=st["x_scales"][:, block(r)],
                rhs=st["x_codes"][:, NODES - width :].bitcast(FP8X4),
                rhs_scale=st["x_scales"][:, NODES - width :],
                start=True,
                stop=True,
            )
            st["cov", r] = cov[:, width - NODES + r * P :]

        def absolute(b, r):
            nc.scalar.activation(
                out=state[b]["result"][:, r, upper(r)], in_=state[b]["cov", r], func=ACT.Abs
            )

        def scale(b, r):
            st = state[b]
            nc.vector.scalar_tensor_tensor(
                out=st["result"][:, r, upper(r)],
                in0=st["result"][:, r, upper(r)],
                scalar=beta_col[:, 0:1],
                in1=st["inv_denom"][:, r, upper(r)],
                op0=ALU.mult,
                op1=ALU.mult,
            )
            store(b, r, slice(r * P, NODES))

        def store(b, r, cols):
            nc.sync.dma_start(out=out[b, r * P : (r + 1) * P, cols], in_=state[b]["result"][:, r, cols])

        def mirror(b, c):
            bank = ps_s.tile([P, c * P], F32, tag="s")
            for r in range(c):
                nc.tensor.transpose(bank[:, block(r)], state[b]["result"][:, r, block(c)], ident[:])
            state[b]["mirror", c] = bank

        def copy_mirror(b, c):
            out_cols = state[b]["result"][:, c, 0 : c * P]
            if b + 1 == GRAPHS and c == 2:
                nc.vector.tensor_copy(out=out_cols, in_=state[b]["mirror", c][:])
            else:
                nc.scalar.copy(out=out_cols, in_=state[b]["mirror", c][:])
            store(b, c, slice(0, c * P))

        def live(b):
            return 0 <= b < GRAPHS

        with tc.manual_schedule(engines={mybir.EngineType.DVE, mybir.EngineType.Activation}):
            for s in range(-3, GRAPHS + 3):
                behind, ahead = s - 1, s + 1
                if live(s + 3) and s < 0:
                    for half in range(2):
                        transpose_h(s + 3, half)
                if live(s - 3):
                    for c in range(1, BLOCKS):
                        copy_mirror(s - 3, c)
                if live(s) and s != TURNED:
                    copy_mean(s)
                    if live(ahead):
                        project_t(s, 2)
                    project_t(s, 3)
                if live(behind):
                    inverse_denominator(behind)
                if live(s + 3) and s >= 0:
                    for half in range(2):
                        transpose_h(s + 3, half)
                if live(behind):
                    for r in range(BLOCKS):
                        absolute(behind, r)
                if live(s) and s != TURNED:
                    centre(s, 0)
                    if live(ahead):
                        mean_and_variance(ahead, 3)
                    for r in range(1, BLOCKS):
                        centre(s, r)
                if live(s + 2):
                    quantise_h(s + 2, 0)
                    if live(ahead) and not (live(s) and s != TURNED):
                        mean_and_variance(ahead, 3)
                    quantise_h(s + 2, 1)
                if live(s - 2):
                    for c in range(1, BLOCKS):
                        mirror(s - 2, c)
                if live(ahead) and ahead != TURNED:
                    spread(ahead, "mean")
                if live(s):
                    inverse_root(s)
                if live(s + 2):
                    for r in range(3):
                        project(s + 2, r)
                    if ahead == TURNED:
                        centre_node(ahead, 3)
                    if live(ahead):
                        inverse_norm(ahead)
                    if live(s):
                        quantise_x(s)
                        for r in range(BLOCKS):
                            covariance(s, r)
                    if live(s + 3):
                        for half in range(2):
                            group_h(s + 3, half)
                    for r in range(BLOCKS):
                        node_stats(s + 2, r)
                        if r == 0:
                            project(s + 2, 3)
                            continue
                        mean_and_variance(s + 2, r - 1)
                        if s + 2 == TURNED:
                            centre_node(s + 2, r - 1)
                        if live(ahead) and ahead != TURNED and r < 3:
                            project_t(ahead, r - 1)
                        if r == 1 and live(ahead):
                            norm(ahead)
                            if ahead == TURNED:
                                for half in range(2):
                                    turn_x(ahead, half)
                    if live(ahead):
                        spread(ahead, "norm")
                    if live(behind):
                        scale(behind, 0)
                    if ahead == TURNED:
                        for half in range(2):
                            group_x(ahead, half)
                    if live(behind):
                        for r in range(1, BLOCKS):
                            scale(behind, r)
                else:
                    if live(ahead):
                        for r in range(3):
                            project_t(ahead, r)
                        inverse_norm(ahead)
                    if live(behind):
                        scale(behind, 0)
                    if live(s):
                        quantise_x(s)
                        for r in range(BLOCKS):
                            covariance(s, r)
                    if live(ahead):
                        norm(ahead)
                        spread(ahead, "norm")
                    if live(behind):
                        for r in range(1, BLOCKS):
                            scale(behind, r)
                    if live(s + 3):
                        for half in range(2):
                            group_h(s + 3, half)
